import numpy as np
import ml_dtypes


def mxq(x, axis, fmt="e4m3"):
    dtype, down = {"e4m3": (ml_dtypes.float8_e4m3fn, 7), "e5m2": (ml_dtypes.float8_e5m2, 14)}[fmt]
    v = np.moveaxis(np.asarray(x, np.float32).astype(ml_dtypes.bfloat16).astype(np.float64), axis, -1)
    blocks = v.reshape(v.shape[:-1] + (-1, 32))
    amax = np.abs(blocks).max(-1, keepdims=True)
    byte = np.maximum(np.where(amax > 0, np.frexp(amax)[1] - 1 + 127, 0) - down, 1)
    scale = np.exp2(byte - 127.0)
    codes = (blocks / scale).astype(np.float32).astype(dtype).astype(np.float64)
    return np.moveaxis((codes * scale).reshape(v.shape), -1, axis)


WIDE = False


def mx_kscale(k):
    if not WIDE:
        return np.ones(k)
    levels = np.array([10, -10, 5, -5, 0])
    if k % 512:
        return np.exp2(np.random.permutation(np.resize(levels, k // 32))).repeat(32)
    a = np.empty((k // 512, 16))
    for p in range(k // 512):
        a[p, :8] = np.random.permutation(np.resize(levels, 8))
        for g in range(8):
            far = levels[np.abs(levels - a[p, g]) >= 10]
            a[p, g + 8] = far[np.random.randint(len(far))]
    return np.exp2(a.ravel()).repeat(32)


BF16 = ml_dtypes.bfloat16


def bf(x):
    return np.asarray(x, np.float32).astype(BF16)


def f64(x):
    return np.asarray(x).astype(np.float64)


B, T, D, H, DK, ROPE, NOPE, VD, KVR, QR = 1, 8192, 512, 2, 128, 64, 64, 128, 512, 1024
EPS = 1.1920928955078125e-07
HALF = ROPE // 2


def rms_norm(h, w):
    var = np.mean(h * h, axis=-1, keepdims=True)
    return h * (1.0 / np.sqrt(var + EPS)) * w


def rope(v):
    inv_freq = 1.0 / (10000.0 ** (f64(np.arange(0, ROPE, 2)) / ROPE))
    freqs = np.outer(f64(np.arange(v.shape[-2])), inv_freq)
    cos, sin = np.cos(freqs), np.sin(freqs)
    v1, v2 = v[..., :HALF], v[..., HALF:]
    return np.concatenate([v1 * cos - v2 * sin, v1 * sin + v2 * cos], axis=-1)


def draw0():
    s, t = mx_kscale(D), mx_kscale(KVR)
    return {'x': bf(np.random.standard_normal((B, T, D)) * s),
            'wkv_c': bf(np.random.standard_normal((D, KVR)) / np.sqrt(D) / s[:, None]),
            'kv_a_norm_w': bf((1.0 + 0.1 * np.random.standard_normal(KVR)) * t),
            'wkv_b': bf(np.random.standard_normal((KVR, H * (NOPE + VD))) / np.sqrt(KVR) / t[:, None]),
            'k_pe': bf(np.random.standard_normal((B, T, ROPE)))}


def core(x, wkv_c, kv_a_norm_w, wkv_b, k_pe):
    c = mxq(f64(x), 2, 'e4m3') @ mxq(f64(wkv_c), 0, 'e4m3')
    cn = rms_norm(c, f64(kv_a_norm_w))
    kv = mxq(cn, 2, 'e4m3') @ mxq(f64(wkv_b), 0, 'e4m3')
    kv = kv.reshape(B, T, H, NOPE + VD).transpose(0, 2, 1, 3)
    k_nope, v = kv[..., :NOPE], kv[..., NOPE:]
    k_rot = rope(f64(k_pe)[:, None])
    k_rot = np.broadcast_to(k_rot, (B, H, T, ROPE))
    ks = np.concatenate([k_nope, k_rot], axis=-1)
    return ks, np.ascontiguousarray(v)


def e4m3fn_bytes(y):
    return np.clip(np.asarray(y, np.float64), -448.0, 448.0).astype(np.float32).astype(ml_dtypes.float8_e4m3fn).view(np.uint8)


def e4m3fn_values(b):
    return np.asarray(b, np.uint8).view(ml_dtypes.float8_e4m3fn).astype(np.float64)


def setup_inputs():
    d = draw0()
    x0 = np.asarray(d['x']).astype(np.float64)
    s = (np.max(np.abs(x0), axis=(0, 1), keepdims=True) / 448.0).astype(np.float32)
    out = {}
    for k, v in d.items():
        if k == 'x':
            out['x_bytes'] = e4m3fn_bytes(x0 / s.astype(np.float64))
            out['x_scale'] = s
        else:
            out[k] = v
    return out


def reference(x_bytes, x_scale, wkv_c, kv_a_norm_w, wkv_b, k_pe):
    return core(e4m3fn_values(x_bytes) * x_scale.astype(np.float64), wkv_c, kv_a_norm_w, wkv_b, k_pe)

@@ -1,0 +1,378 @@
+import math
+from contextlib import ExitStack
+
+import concourse.mybir as mybir
+from concourse.masks import make_identity
+
+F32 = mybir.dt.float32
+BF16 = mybir.dt.bfloat16
+I32 = mybir.dt.int32
+U32 = mybir.dt.uint32
+U8 = mybir.dt.uint8
+FP8 = mybir.dt.float8_e4m3fn
+FP8X4 = mybir.dt.float8_e4m3fn_x4
+ALU = mybir.AluOpType
+ACT = mybir.ActivationFunctionType
+
+P = 128
+T, D, KVR, H, NOPE, ROPE, VD = 8192, 512, 512, 2, 64, 64, 128
+HALF = ROPE // 2
+EPS = 1.1920928955078125e-07
+FLOPS = 2 * T * D * KVR + 2 * T * KVR * H * (NOPE + VD)
+
+SLOTS = T // P
+PAIR = 2
+UNITS = SLOTS // PAIR
+OCT = 8
+LOADS = [2, 2, 4] + [8] * 7
+
+
+def turns(x):
+    return x - math.floor(x + 0.5)
+
+
+def tile_deepseekmultiheadattention_pb_t_kernel(
+    tc, x_bytes, x_scale, wkv_c, kv_a_norm_w, wkv_b, k_pe, out_0, out_1
+):
+    nc = tc.nc
+    with ExitStack() as ctx:
+        keep = ctx.enter_context(tc.tile_pool(name="keep", bufs=1))
+        work = ctx.enter_context(tc.tile_pool(name="work", bufs=3))
+        psum = ctx.enter_context(tc.psum_pool(name="psum", bufs=1))
+        ctx.enter_context(tc.manual_schedule())
+
+        xview = x_bytes.rearrange("o (p i) k -> p (o i k)", p=P)
+        scale_rep = keep.tile([P, PAIR * D], F32, name="scale_rep", align_bytes=64)
+        nc.sync.dma_start(
+            out=scale_rep[:, 0:D], in_=x_scale.rearrange("a b k -> (a b k)").partition_broadcast(P)
+        )
+        wc_raw = keep.tile([P, 4, KVR], BF16, name="wc_raw", align_bytes=64)
+        nc.scalar.dma_start(out=wc_raw[:], in_=wkv_c.rearrange("(p j) n -> p j n", j=4))
+
+        xb = []
+        first = []
+        start = 0
+        for g, n in enumerate(LOADS):
+            t = keep.tile([P, n * D], U8, name="xb%d" % g, align_bytes=64)
+            xb.append(t)
+            first.append(start)
+            start += n
+        kp = keep.tile([P, SLOTS, ROPE], BF16, name="kp", align_bytes=64)
+        kpview = k_pe.rearrange("o (p i) r -> p (o i) r", p=P)
+        wb_raw = keep.tile([P, 4, H * (NOPE + VD)], BF16, name="wb_raw", align_bytes=64)
+        gain_raw = keep.tile([P, KVR], BF16, name="gain_raw", align_bytes=64)
+
+        def load_x(g):
+            nc.sync.dma_start(out=xb[g][:], in_=xview[:, first[g] * D : (first[g] + LOADS[g]) * D])
+
+        load_x(0)
+        load_x(1)
+        nc.sync.dma_start(out=gain_raw[:], in_=kv_a_norm_w.partition_broadcast(P))
+        load_x(2)
+        nc.sync.dma_start(out=wb_raw[:], in_=wkv_b.rearrange("(p j) n -> p j n", j=4))
+        load_x(3)
+        nc.sync.dma_start(out=kp[:, 0:32, :], in_=kpview[:, 0:32, :])
+        load_x(4)
+        nc.sync.dma_start(out=kp[:, 32:64, :], in_=kpview[:, 32:64, :])
+        for g in range(5, len(LOADS)):
+            load_x(g)
+
+        ident = keep.tile([P, P], F32, name="ident")
+        make_identity(nc, ident[:])
+        zeros = keep.tile([P, 2], F32, name="zeros")
+        nc.vector.memset(zeros[:], 0.0)
+        freq = keep.tile([P, 2, P], F32, name="freq")
+        nc.vector.memset(freq[:, 0, :], 0.0)
+        nc.gpsimd.memset(freq[:, 1, :], 0.0)
+        nhalf = keep.tile([P, PAIR], F32, name="nhalf")
+        nc.gpsimd.memset(nhalf[:], -0.5)
+        for j in range(HALF):
+            w = 10000.0 ** (-j / HALF) / (2.0 * math.pi)
+            nc.vector.tensor_scalar(
+                out=freq[:, 0, j : 2 * HALF : HALF], in0=zeros[:], scalar1=1.0, scalar2=turns(SLOTS * w),
+                op0=ALU.mult, op1=ALU.add,
+            )
+            nc.gpsimd.tensor_scalar(
+                out=freq[:, 1, j : 2 * HALF : HALF], in0=zeros[:], scalar1=1.0, scalar2=turns(w),
+                op0=ALU.mult, op1=ALU.add,
+            )
+        ramp = keep.tile([P, P], F32, name="ramp")
+        nc.gpsimd.iota(
+            ramp[:], pattern=[[1, P]], base=0, channel_multiplier=0, allow_small_or_imprecise_dtypes=True
+        )
+        phase = keep.tile([P, 3], F32, name="phase")
+        nc.gpsimd.memset(phase[:], 0.0)
+        nc.gpsimd.memset(phase[0:32, 0:2], 0.25)
+        nc.gpsimd.memset(phase[32:64, 1:2], 0.5)
+        nc.gpsimd.memset(phase[32:64, 2:3], 0.25)
+        mask = keep.tile([P, HALF], F32, name="mask")
+        trig = keep.tile([P, 256], F32, name="trig")
+        gain = keep.tile([P, KVR], BF16, name="gain")
+
+        wc_il = keep.tile([P, KVR, 4], BF16, name="wc_il", align_bytes=64)
+        wc_q = keep.tile([P, KVR], U32, name="wc_q", align_bytes=64)
+        wc_s = keep.tile([P, KVR], U8, name="wc_s", align_bytes=64)
+        wb_il = keep.tile([P, 384, 4], BF16, name="wb_il", align_bytes=64)
+        wb_q = keep.tile([P, 384], U32, name="wb_q", align_bytes=64)
+        wb_s = keep.tile([P, 384], U8, name="wb_s", align_bytes=64)
+
+        def quantize(codes, scales, src):
+            nc.vector.quantize_mx(out=codes.bitcast(FP8X4), scales=scales, in_=src)
+
+        def wc_interleave(copy, u):
+            copy(
+                out=wc_il[:, u * 256 : (u + 1) * 256, :].rearrange("p (m e) j -> p m e j", e=2),
+                in_=wc_raw[:].rearrange("p j (m u e) -> p u m e j", u=2, e=2)[:, u],
+            )
+
+        def wc_quantize(u):
+            cols = slice(u * 256, (u + 1) * 256)
+            quantize(wc_q[:, cols], wc_s[:, cols], wc_il[:, cols, :].rearrange("p n j -> p (n j)"))
+
+        def wb_interleave():
+            by_head = wb_raw[:].rearrange("p j (h c) -> p h c j", h=H)
+            nc.scalar.copy(
+                out=wb_il[:, 0:256, :].rearrange("p (h c) j -> p h c j", h=H), in_=by_head[:, :, NOPE:, :]
+            )
+            nc.scalar.copy(
+                out=wb_il[:, 256:384, :].rearrange("p (h c) j -> p h c j", h=H), in_=by_head[:, :, 0:NOPE, :]
+            )
+
+        def wb_quantize():
+            quantize(wb_q[:, 0:256], wb_s[:, 0:256], wb_il[:, 0:256, :].rearrange("p n j -> p (n j)"))
+            quantize(wb_q[:, 256:384], wb_s[:, 256:384], wb_il[:, 256:384, :].rearrange("p n j -> p (n j)"))
+
+        def trig_tables():
+            nc.vector.tensor_tensor(out=mask[:], in0=ident[:, 0:HALF], in1=ident[:, HALF : 2 * HALF], op=ALU.add)
+            col = psum.tile([P, 512], F32, name="kvn")
+            nc.tensor.transpose(col[:, 0:P], freq[:, 0, :], ident[:])
+            nc.tensor.transpose(col[:, P : 2 * P], freq[:, 1, :], ident[:])
+            wcol = keep.tile([P, 2], F32, name="wcol")
+            nc.vector.tensor_copy(out=wcol[:], in_=col[:, 0 : 2 * P : P])
+            arg = keep.tile([P, 256], F32, name="arg")
+            argi = keep.tile([P, 256], I32, name="argi")
+            frac = keep.tile([P, 256], F32, name="frac")
+            for lo, hi, wi, ph in ((0, 128, 0, 0), (128, 192, 1, 1), (192, 256, 1, 2)):
+                nc.vector.tensor_scalar(
+                    out=arg[:, lo:hi], in0=ramp[:, 0 : hi - lo], scalar1=wcol[:, wi : wi + 1],
+                    scalar2=phase[:, ph : ph + 1], op0=ALU.mult, op1=ALU.add,
+                )
+            nc.vector.tensor_copy(out=argi[:], in_=arg[:])
+            nc.vector.tensor_tensor(out=frac[:], in0=arg[:], in1=argi[:], op=ALU.subtract)
+            nc.scalar.activation(out=trig[:], in_=frac[:], func=ACT.Sin, scale=2.0 * math.pi)
+
+        xs, xw, xg, xq, xsc = {}, {}, {}, {}, {}
+        cb, ssq, rr, cnb, cw, cg, cq, csc = {}, {}, {}, {}, {}, {}, {}, {}
+        kvv, kvn, kst, vst = {}, {}, {}, {}
+
+        def x_scale_mul(u):
+            g = max(i for i in range(len(LOADS)) if first[i] <= PAIR * u)
+            off = (PAIR * u - first[g]) * D
+            xs[u] = work.tile([P, PAIR * D], BF16, name="xs", align_bytes=64)
+            step = D if u == 0 else PAIR * D
+            for lo in range(0, PAIR * D, step):
+                nc.vector.tensor_tensor(
+                    out=xs[u][:, lo : lo + step], in0=xb[g][:, off + lo : off + lo + step].bitcast(FP8),
+                    in1=scale_rep[:, 0:step], op=ALU.mult,
+                )
+
+        def x_transpose(u):
+            xw[u] = psum.tile([P, 4, P], F32, name="xw")
+            words = xs[u][:].bitcast(F32)
+            for a in range(PAIR):
+                for e in range(2):
+                    nc.tensor.transpose(
+                        xw[u][:, 2 * a + e, :], words[:, a * 256 + e : (a + 1) * 256 : 2], ident[:]
+                    )
+
+        def evac_words(dst, src):
+            nc.scalar.copy(
+                out=dst.bitcast(F32).rearrange("p (a r u) -> p a r u", a=PAIR, u=2),
+                in_=src.rearrange("p (a u) r -> p a r u", a=PAIR),
+            )
+
+        def x_evac(u):
+            xg[u] = work.tile([P, PAIR * D], BF16, name="xg", align_bytes=64)
+            evac_words(xg[u][:], xw[u][:])
+
+        def x_quantize(u):
+            xq[u] = work.tile([P, 256], U32, name="xq", align_bytes=64)
+            xsc[u] = work.tile([P, 256], U8, name="xsc", align_bytes=64)
+            quantize(xq[u][:], xsc[u][:], xg[u][:])
+
+        def mx(out, lq, ls, lcols, rq, rs, rcols):
+            nc.tensor.matmul_mx(
+                out=out, lhsT=lq[:, lcols].bitcast(FP8X4), lhsT_scale=ls[:, lcols],
+                rhs=rq[:, rcols].bitcast(FP8X4), rhs_scale=rs[:, rcols], start=True, stop=True,
+            )
+
+        def mx1(u):
+            cb[u] = []
+            for a in range(PAIR):
+                c = psum.tile([P, KVR], F32, name="c", bufs=4)
+                mx(c[:], xq[u], xsc[u], slice(a * P, (a + 1) * P), wc_q, wc_s, slice(0, KVR))
+                cb[u].append(c)
+
+        def squares(u):
+            ssq[u] = work.tile([P, PAIR], F32, name="ssq")
+            for a in range(PAIR):
+                junk = work.tile([P, KVR], BF16, name="junk")
+                nc.scalar.activation(
+                    out=junk[:], in_=cb[u][a][:], func=ACT.Square, accum_out=ssq[u][:, a : a + 1]
+                )
+
+        def rnorm(u):
+            ms = work.tile([P, PAIR], F32, name="ms")
+            rr[u] = work.tile([P, PAIR], F32, name="rr")
+            nc.gpsimd.tensor_scalar(
+                out=ms[:], in0=ssq[u][:], scalar1=1.0 / KVR, scalar2=EPS, op0=ALU.mult, op1=ALU.add
+            )
+            nc.gpsimd.tensor_tensor(out=rr[u][:], in0=ms[:], in1=nhalf[:], op=ALU.pow)
+
+        def c_norm(u):
+            cnb[u] = work.tile([P, PAIR * KVR], BF16, name="cnb", align_bytes=64)
+            for a in range(PAIR):
+                nc.vector.scalar_tensor_tensor(
+                    out=cnb[u][:, a * KVR : (a + 1) * KVR], in0=cb[u][a][:], scalar=rr[u][:, a : a + 1],
+                    in1=gain[:], op0=ALU.mult, op1=ALU.mult,
+                )
+
+        def c_transpose(u):
+            cw[u] = psum.tile([P, 4, P], F32, name="cw")
+            words = cnb[u][:].bitcast(F32)
+            for b in range(4):
+                nc.tensor.transpose(cw[u][:, b, :], words[:, b * P : (b + 1) * P], ident[:])
+
+        def c_evac(u):
+            cg[u] = work.tile([P, PAIR * KVR], BF16, name="cg", align_bytes=64)
+            evac_words(cg[u][:], cw[u][:])
+
+        def c_quantize(u):
+            cq[u] = work.tile([P, 256], U32, name="cq", align_bytes=64)
+            csc[u] = work.tile([P, 256], U8, name="csc", align_bytes=64)
+            quantize(cq[u][:], csc[u][:], cg[u][:])
+
+        def mx2(u):
+            kvv[u] = psum.tile([P, PAIR, 256], F32, name="kvv")
+            kvn[u] = psum.tile([P, 512], F32, name="kvn")
+            for a in range(PAIR):
+                cols = slice(a * P, (a + 1) * P)
+                mx(kvv[u][:, a, :], cq[u], csc[u], cols, wb_q, wb_s, slice(0, 256))
+                mx(kvn[u][:, a * P : (a + 1) * P], cq[u], csc[u], cols, wb_q, wb_s, slice(256, 384))
+
+        def out_tiles(q):
+            if q not in kst:
+                kst[q] = work.tile([P, OCT, 192], F32, name="kst")
+                vst[q] = work.tile([P, H, OCT, VD], F32, name="vst")
+            return kst[q], vst[q]
+
+        def kv_evac(u):
+            kt, vt = out_tiles(u // 4)
+            i0 = PAIR * (u % 4)
+            nc.scalar.copy(
+                out=vt[:, :, i0 : i0 + PAIR, :].rearrange("p h i d -> p i h d"),
+                in_=kvv[u][:].rearrange("p i (h d) -> p i h d", h=H),
+            )
+            copy = nc.vector.tensor_copy if u == UNITS - 1 else nc.scalar.copy
+            copy(
+                out=kt[:, i0 : i0 + PAIR, :].rearrange("p i (s d) -> p i s d", s=3)[:, :, 0:3:2, :],
+                in_=kvn[u][:, 0:256].rearrange("p (i h d) -> p i h d", i=PAIR, h=H),
+            )
+
+        o0 = out_0.rearrange("o h (p i) d -> (o h) p i d", p=P)
+        o1 = out_1.rearrange("o h (p i) d -> p (o h) i d", p=P)
+
+        def store(u):
+            q = u // 4
+            if q == UNITS // 4 - 1:
+                lo, n = PAIR * (u % 4), PAIR
+            elif u % 4 == 3:
+                lo, n = 0, OCT
+            else:
+                return
+            kt, vt = out_tiles(q)
+            i0 = q * OCT + lo
+            nc.sync.dma_start(out=o1[:, :, i0 : i0 + n, :], in_=vt[:, :, lo : lo + n, :])
+            nc.sync.dma_start(out=o0[0][:, i0 : i0 + n, :], in_=kt[:, lo : lo + n, 0:128])
+            nc.sync.dma_start(out=o0[1][:, i0 : i0 + n, 0:64], in_=kt[:, lo : lo + n, 128:192])
+            nc.sync.dma_start(out=o0[1][:, i0 : i0 + n, 64:128], in_=kt[:, lo : lo + n, 64:128])
+
+        prod = {}
+
+        def rope_step(s, bank):
+            q, which = s // 2, s % 2
+            rhs = work.tile([P, OCT, HALF], F32, name="rhs")
+            t0 = P + 64 * which + q * OCT
+            nc.gpsimd.tensor_tensor(
+                out=rhs[:], in0=trig[:, t0 : t0 + OCT].unsqueeze(2).to_broadcast([P, OCT, HALF]),
+                in1=mask[:].unsqueeze(1).to_broadcast([P, OCT, HALF]), op=ALU.mult,
+            )
+            nc.tensor.matmul(
+                out=bank[:, 256:512], lhsT=trig[:, 0:P], rhs=rhs[:].rearrange("p i j -> p (i j)"),
+                start=True, stop=True,
+            )
+            m = work.tile([P, OCT, 2, HALF], F32, name="prod%d" % which)
+            prod[which] = m
+            nc.vector.tensor_tensor(
+                out=m[:], in0=kp[:, q * OCT : (q + 1) * OCT, :].rearrange("p i (s j) -> p i s j", s=2),
+                in1=bank[:, 256:512].rearrange("p (i j) -> p i j", j=HALF).unsqueeze(2).to_broadcast([P, OCT, 2, HALF]),
+                op=ALU.mult,
+            )
+            if which == 1:
+                kt, vt = out_tiles(q)
+                nc.vector.tensor_tensor(
+                    out=kt[:, :, 64:96], in0=prod[0][:, :, 0, :], in1=prod[1][:, :, 1, :], op=ALU.subtract
+                )
+                nc.vector.tensor_tensor(
+                    out=kt[:, :, 96:128], in0=prod[0][:, :, 1, :], in1=prod[1][:, :, 0, :], op=ALU.add
+                )
+
+        rope_at = {2 + (s * 7) // 4: s for s in range(16)}
+
+        def ok(u):
+            return 0 <= u < UNITS
+
+        for n in range(-4, UNITS + 2):
+            if ok(n + 3):
+                x_transpose(n + 3)
+            if ok(n + 1):
+                squares(n + 1)
+                rnorm(n + 1)
+            if ok(n - 2):
+                kv_evac(n - 2)
+                store(n - 2)
+            if ok(n):
+                c_norm(n)
+                c_transpose(n)
+            if ok(n + 3):
+                x_evac(n + 3)
+            if ok(n):
+                c_evac(n)
+            if ok(n + 2):
+                x_quantize(n + 2)
+            if ok(n - 1):
+                c_quantize(n - 1)
+            if n == -3:
+                wc_quantize(0)
+                wc_quantize(1)
+            if ok(n + 2):
+                mx1(n + 2)
+            if ok(n - 1):
+                mx2(n - 1)
+            if ok(n + 4):
+                x_scale_mul(n + 4)
+            if n == -4:
+                nc.scalar.copy(out=scale_rep[:, D : 2 * D], in_=scale_rep[:, 0:D])
+                wc_interleave(nc.vector.tensor_copy, 0)
+                wc_interleave(nc.scalar.copy, 1)
+                nc.gpsimd.tensor_copy(
+                    out=gain[:].rearrange("p (u m e) -> p u m e", u=2, e=2),
+                    in_=gain_raw[:].rearrange("p (m u e) -> p u m e", u=2, e=2),
+                )
+            if n == -2:
+                wb_interleave()
+            if n == -1:
+                wb_quantize()
+                trig_tables()
+            if n in rope_at:
+                rope_step(rope_at[n], kvn[n - 1])

@@ -82,19 +82,15 @@ def tile_deepseekmultiheadattention_pb_t_kernel(
         zeros = keep.tile([P, 2], F32, name="zeros")
         nc.vector.memset(zeros[:], 0.0)
         freq = keep.tile([P, 2, P], F32, name="freq")
-        nc.vector.memset(freq[:, 0, :], 0.0)
-        nc.gpsimd.memset(freq[:, 1, :], 0.0)
-        nhalf = keep.tile([P, PAIR], F32, name="nhalf")
-        nc.gpsimd.memset(nhalf[:], -0.5)
+        nc.vector.memset(freq[:], 0.0)
         for j in range(HALF):
             w = 10000.0 ** (-j / HALF) / (2.0 * math.pi)
             nc.vector.tensor_scalar(
                 out=freq[:, 0, j : 2 * HALF : HALF], in0=zeros[:], scalar1=1.0, scalar2=turns(SLOTS * w),
                 op0=ALU.mult, op1=ALU.add,
             )
-            nc.gpsimd.tensor_scalar(
-                out=freq[:, 1, j : 2 * HALF : HALF], in0=zeros[:], scalar1=1.0, scalar2=turns(w),
-                op0=ALU.mult, op1=ALU.add,
+            nc.scalar.activation(
+                out=freq[:, 1, j : 2 * HALF : HALF], in_=zeros[:], func=ACT.Copy, bias=turns(w)
             )
         ramp = keep.tile([P, P], F32, name="ramp")
         nc.gpsimd.iota(
@@ -102,11 +98,12 @@ def tile_deepseekmultiheadattention_pb_t_kernel(
         )
         phase = keep.tile([P, 3], F32, name="phase")
         nc.gpsimd.memset(phase[:], 0.0)
-        nc.gpsimd.memset(phase[0:32, 0:2], 0.25)
-        nc.gpsimd.memset(phase[32:64, 1:2], 0.5)
-        nc.gpsimd.memset(phase[32:64, 2:3], 0.25)
+        nc.gpsimd.memset(phase[0:32, 0:1], 0.25)
+        nc.gpsimd.memset(phase[32:64, 1:2], -0.25)
+        nc.gpsimd.memset(phase[0:32, 2:3], 0.25)
+        nc.gpsimd.memset(phase[32:64, 2:3], 0.5)
         mask = keep.tile([P, HALF], F32, name="mask")
-        trig = keep.tile([P, 256], F32, name="trig")
+        trig = keep.tile([P, 320], F32, name="trig")
         gain = keep.tile([P, KVR], BF16, name="gain")
 
         wc_il = keep.tile([P, KVR, 4], BF16, name="wc_il", align_bytes=64)
@@ -149,10 +146,10 @@ def tile_deepseekmultiheadattention_pb_t_kernel(
             nc.tensor.transpose(col[:, P : 2 * P], freq[:, 1, :], ident[:])
             wcol = keep.tile([P, 2], F32, name="wcol")
             nc.vector.tensor_copy(out=wcol[:], in_=col[:, 0 : 2 * P : P])
-            arg = keep.tile([P, 256], F32, name="arg")
-            argi = keep.tile([P, 256], I32, name="argi")
-            frac = keep.tile([P, 256], F32, name="frac")
-            for lo, hi, wi, ph in ((0, 128, 0, 0), (128, 192, 1, 1), (192, 256, 1, 2)):
+            arg = keep.tile([P, 320], F32, name="arg")
+            argi = keep.tile([P, 320], I32, name="argi")
+            frac = keep.tile([P, 320], F32, name="frac")
+            for lo, hi, wi, ph in ((0, 128, 0, 0), (128, 256, 0, 1), (256, 320, 1, 2)):
                 nc.vector.tensor_scalar(
                     out=arg[:, lo:hi], in0=ramp[:, 0 : hi - lo], scalar1=wcol[:, wi : wi + 1],
                     scalar2=phase[:, ph : ph + 1], op0=ALU.mult, op1=ALU.add,
@@ -222,12 +219,10 @@ def tile_deepseekmultiheadattention_pb_t_kernel(
                 )
 
         def rnorm(u):
-            ms = work.tile([P, PAIR], F32, name="ms")
             rr[u] = work.tile([P, PAIR], F32, name="rr")
-            nc.gpsimd.tensor_scalar(
-                out=ms[:], in0=ssq[u][:], scalar1=1.0 / KVR, scalar2=EPS, op0=ALU.mult, op1=ALU.add
+            nc.scalar.activation(
+                out=rr[u][:], in_=ssq[u][:], func=ACT.Abs_reciprocal_sqrt, scale=1.0 / KVR, bias=EPS
             )
-            nc.gpsimd.tensor_tensor(out=rr[u][:], in0=ms[:], in1=nhalf[:], op=ALU.pow)
 
         def c_norm(u):
             cnb[u] = work.tile([P, PAIR * KVR], BF16, name="cnb", align_bytes=64)
@@ -297,19 +292,21 @@ def tile_deepseekmultiheadattention_pb_t_kernel(
             nc.sync.dma_start(out=o0[1][:, i0 : i0 + n, 0:64], in_=kt[:, lo : lo + n, 128:192])
             nc.sync.dma_start(out=o0[1][:, i0 : i0 + n, 64:128], in_=kt[:, lo : lo + n, 64:128])
 
-        prod = {}
+        prod, rhs = {}, {}
+
+        def rope_rhs(q):
+            rhs[q] = work.tile([P, OCT, HALF], F32, name="rhs")
+            t0 = 2 * P + q * OCT
+            nc.vector.tensor_tensor(
+                out=rhs[q][:], in0=trig[:, t0 : t0 + OCT].unsqueeze(2).to_broadcast([P, OCT, HALF]),
+                in1=mask[:].unsqueeze(1).to_broadcast([P, OCT, HALF]), op=ALU.mult,
+            )
 
         def rope_step(s, bank):
             q, which = s // 2, s % 2
-            rhs = work.tile([P, OCT, HALF], F32, name="rhs")
-            t0 = P + 64 * which + q * OCT
-            nc.gpsimd.tensor_tensor(
-                out=rhs[:], in0=trig[:, t0 : t0 + OCT].unsqueeze(2).to_broadcast([P, OCT, HALF]),
-                in1=mask[:].unsqueeze(1).to_broadcast([P, OCT, HALF]), op=ALU.mult,
-            )
             nc.tensor.matmul(
-                out=bank[:, 256:512], lhsT=trig[:, 0:P], rhs=rhs[:].rearrange("p i j -> p (i j)"),
-                start=True, stop=True,
+                out=bank[:, 256:512], lhsT=trig[:, which * P : (which + 1) * P],
+                rhs=rhs[q][:].rearrange("p i j -> p (i j)"), start=True, stop=True,
             )
             m = work.tile([P, OCT, 2, HALF], F32, name="prod%d" % which)
             prod[which] = m
@@ -328,6 +325,7 @@ def tile_deepseekmultiheadattention_pb_t_kernel(
                 )
 
         rope_at = {2 + (s * 7) // 4: s for s in range(16)}
+        rhs_at = {1 + (2 * q * 7) // 4: q for q in range(8)}
 
         def ok(u):
             return 0 <= u < UNITS
@@ -337,10 +335,11 @@ def tile_deepseekmultiheadattention_pb_t_kernel(
                 x_transpose(n + 3)
             if ok(n + 1):
                 squares(n + 1)
-                rnorm(n + 1)
             if ok(n - 2):
                 kv_evac(n - 2)
                 store(n - 2)
+            if ok(n + 1):
+                rnorm(n + 1)
             if ok(n):
                 c_norm(n)
                 c_transpose(n)
@@ -365,7 +364,7 @@ def tile_deepseekmultiheadattention_pb_t_kernel(
                 nc.scalar.copy(out=scale_rep[:, D : 2 * D], in_=scale_rep[:, 0:D])
                 wc_interleave(nc.vector.tensor_copy, 0)
                 wc_interleave(nc.scalar.copy, 1)
-                nc.gpsimd.tensor_copy(
+                nc.scalar.copy(
                     out=gain[:].rearrange("p (u m e) -> p u m e", u=2, e=2),
                     in_=gain_raw[:].rearrange("p (m u e) -> p u m e", u=2, e=2),
                 )
@@ -374,5 +373,7 @@ def tile_deepseekmultiheadattention_pb_t_kernel(
             if n == -1:
                 wb_quantize()
                 trig_tables()
+            if n in rhs_at:
+                rope_rhs(rhs_at[n])
             if n in rope_at:
                 rope_step(rope_at[n], kvn[n - 1])

@@ -81,6 +81,8 @@ def tile_deepseekmultiheadattention_pb_t_kernel(
         make_identity(nc, ident[:])
         zeros = keep.tile([P, 2], F32, name="zeros")
         nc.vector.memset(zeros[:], 0.0)
+        nhalf = keep.tile([P, 1], F32, name="nhalf")
+        nc.gpsimd.memset(nhalf[:], 1.0)
         freq = keep.tile([P, 2, P], F32, name="freq")
         nc.vector.memset(freq[:], 0.0)
         for j in range(HALF):
@@ -293,6 +295,8 @@ def tile_deepseekmultiheadattention_pb_t_kernel(
             nc.sync.dma_start(out=o0[1][:, i0 : i0 + n, 64:128], in_=kt[:, lo : lo + n, 64:128])
 
         prod, rhs = {}, {}
+        STEPS = 2 * SLOTS // OCT
+        step_at = {(7 * s) // 4: s for s in range(STEPS)}
 
         def rope_rhs(q):
             rhs[q] = work.tile([P, OCT, HALF], F32, name="rhs")
@@ -302,78 +306,73 @@ def tile_deepseekmultiheadattention_pb_t_kernel(
                 in1=mask[:].unsqueeze(1).to_broadcast([P, OCT, HALF]), op=ALU.mult,
             )
 
-        def rope_step(s, bank):
-            q, which = s // 2, s % 2
+        def rope_table(u):
+            if u not in step_at:
+                return
+            q, which = step_at[u] // 2, step_at[u] % 2
             nc.tensor.matmul(
-                out=bank[:, 256:512], lhsT=trig[:, which * P : (which + 1) * P],
+                out=kvn[u][:, 256:512], lhsT=trig[:, which * P : (which + 1) * P],
                 rhs=rhs[q][:].rearrange("p i j -> p (i j)"), start=True, stop=True,
             )
+
+        def rope_products(u):
+            if u not in step_at:
+                return
+            q, which = step_at[u] // 2, step_at[u] % 2
             m = work.tile([P, OCT, 2, HALF], F32, name="prod%d" % which)
             prod[which] = m
             nc.vector.tensor_tensor(
                 out=m[:], in0=kp[:, q * OCT : (q + 1) * OCT, :].rearrange("p i (s j) -> p i s j", s=2),
-                in1=bank[:, 256:512].rearrange("p (i j) -> p i j", j=HALF).unsqueeze(2).to_broadcast([P, OCT, 2, HALF]),
+                in1=kvn[u][:, 256:512].rearrange("p (i j) -> p i j", j=HALF).unsqueeze(2).to_broadcast([P, OCT, 2, HALF]),
                 op=ALU.mult,
             )
             if which == 1:
                 kt, vt = out_tiles(q)
-                nc.vector.tensor_tensor(
+                nc.gpsimd.tensor_tensor(
                     out=kt[:, :, 64:96], in0=prod[0][:, :, 0, :], in1=prod[1][:, :, 1, :], op=ALU.subtract
                 )
-                nc.vector.tensor_tensor(
+                nc.gpsimd.tensor_tensor(
                     out=kt[:, :, 96:128], in0=prod[0][:, :, 1, :], in1=prod[1][:, :, 0, :], op=ALU.add
                 )
+            elif q + 1 < SLOTS // OCT:
+                rope_rhs(q + 1)
 
-        rope_at = {2 + (s * 7) // 4: s for s in range(16)}
-        rhs_at = {1 + (2 * q * 7) // 4: q for q in range(8)}
-
-        def ok(u):
-            return 0 <= u < UNITS
-
-        for n in range(-4, UNITS + 2):
-            if ok(n + 3):
-                x_transpose(n + 3)
-            if ok(n + 1):
-                squares(n + 1)
-            if ok(n - 2):
-                kv_evac(n - 2)
-                store(n - 2)
-            if ok(n + 1):
-                rnorm(n + 1)
-            if ok(n):
-                c_norm(n)
-                c_transpose(n)
-            if ok(n + 3):
-                x_evac(n + 3)
-            if ok(n):
-                c_evac(n)
-            if ok(n + 2):
-                x_quantize(n + 2)
-            if ok(n - 1):
-                c_quantize(n - 1)
+        stages = [
+            (c_transpose, -1),
+            (x_scale_mul, 3),
+            (c_quantize, -2),
+            (mx1, 1),
+            (rope_products, -3),
+            (x_transpose, 3),
+            (kv_evac, -3),
+            (store, -3),
+            (c_evac, -1),
+            (c_norm, 0),
+            (squares, 1),
+            (x_quantize, 2),
+            (rnorm, 1),
+            (mx2, -2),
+            (rope_table, -2),
+            (x_evac, 3),
+        ]
+        nc.scalar.copy(out=scale_rep[:, D : 2 * D], in_=scale_rep[:, 0:D])
+        wc_interleave(nc.scalar.copy, 1)
+        for n in range(-3, UNITS + 3):
+            for stage, lag in stages:
+                if 0 <= n + lag < UNITS:
+                    stage(n + lag)
             if n == -3:
-                wc_quantize(0)
-                wc_quantize(1)
-            if ok(n + 2):
-                mx1(n + 2)
-            if ok(n - 1):
-                mx2(n - 1)
-            if ok(n + 4):
-                x_scale_mul(n + 4)
-            if n == -4:
-                nc.scalar.copy(out=scale_rep[:, D : 2 * D], in_=scale_rep[:, 0:D])
                 wc_interleave(nc.vector.tensor_copy, 0)
-                wc_interleave(nc.scalar.copy, 1)
+                trig_tables()
+                nc.scalar.activation(out=zeros[:, 0:1], in_=nhalf[:, 0:1], func=ACT.Abs_reciprocal_sqrt)
                 nc.scalar.copy(
                     out=gain[:].rearrange("p (u m e) -> p u m e", u=2, e=2),
                     in_=gain_raw[:].rearrange("p (m u e) -> p u m e", u=2, e=2),
                 )
             if n == -2:
+                wc_quantize(0)
+                wc_quantize(1)
                 wb_interleave()
             if n == -1:
                 wb_quantize()
-                trig_tables()
-            if n in rhs_at:
-                rope_rhs(rhs_at[n])
-            if n in rope_at:
-                rope_step(rope_at[n], kvn[n - 1])
+                rope_rhs(0)

@@ -24,6 +24,7 @@ SLOTS = T // P
 PAIR = 2
 UNITS = SLOTS // PAIR
 OCT = 8
+QUAD = 4
 LOADS = [2, 2, 4] + [8] * 7
 
 
@@ -79,21 +80,30 @@ def tile_deepseekmultiheadattention_pb_t_kernel(
 
         ident = keep.tile([P, P], F32, name="ident")
         make_identity(nc, ident[:])
-        zeros = keep.tile([P, 2], F32, name="zeros")
-        nc.vector.memset(zeros[:], 0.0)
-        nhalf = keep.tile([P, 1], F32, name="nhalf")
-        nc.gpsimd.memset(nhalf[:], 1.0)
+        ones = keep.tile([P, 1], F32, name="ones")
+        nc.vector.memset(ones[:], 1.0)
+        warm = keep.tile([P, 1], F32, name="warm")
+        nc.scalar.activation(out=warm[:], in_=ones[:], func=ACT.Sin)
         freq = keep.tile([P, 2, P], F32, name="freq")
         nc.vector.memset(freq[:], 0.0)
-        for j in range(HALF):
-            w = 10000.0 ** (-j / HALF) / (2.0 * math.pi)
+        for j in range(8):
             nc.vector.tensor_scalar(
-                out=freq[:, 0, j : 2 * HALF : HALF], in0=zeros[:], scalar1=1.0, scalar2=turns(SLOTS * w),
-                op0=ALU.mult, op1=ALU.add,
+                out=freq[:, 1, j : j + 1], in0=ones[:], scalar1=10000.0 ** (-j / HALF) / (2.0 * math.pi),
+                scalar2=None, op0=ALU.mult,
             )
-            nc.scalar.activation(
-                out=freq[:, 1, j : 2 * HALF : HALF], in_=zeros[:], func=ACT.Copy, bias=turns(w)
+        for j in range(11):
+            nc.vector.tensor_scalar(
+                out=freq[:, 0, j : j + 1], in0=ones[:],
+                scalar1=turns(SLOTS * 10000.0 ** (-j / HALF) / (2.0 * math.pi)), scalar2=None, op0=ALU.mult,
             )
+        for w, f in ((8, 0.1), (16, 0.01)):
+            nc.vector.tensor_scalar(
+                out=freq[:, 1, w : 2 * w], in0=freq[:, 1, 0:w], scalar1=f, scalar2=None, op0=ALU.mult
+            )
+        nc.vector.tensor_scalar(
+            out=freq[:, 0, 11:HALF], in0=freq[:, 1, 11:HALF], scalar1=float(SLOTS), scalar2=None, op0=ALU.mult
+        )
+        nc.vector.tensor_copy(out=freq[:, :, HALF : 2 * HALF], in_=freq[:, :, 0:HALF])
         ramp = keep.tile([P, P], F32, name="ramp")
         nc.gpsimd.iota(
             ramp[:], pattern=[[1, P]], base=0, channel_multiplier=0, allow_small_or_imprecise_dtypes=True
@@ -107,6 +117,7 @@ def tile_deepseekmultiheadattention_pb_t_kernel(
         mask = keep.tile([P, HALF], F32, name="mask")
         trig = keep.tile([P, 320], F32, name="trig")
         gain = keep.tile([P, KVR], BF16, name="gain")
+        frac = keep.tile([P, 320], F32, name="frac")
 
         wc_il = keep.tile([P, KVR, 4], BF16, name="wc_il", align_bytes=64)
         wc_q = keep.tile([P, KVR], U32, name="wc_q", align_bytes=64)
@@ -130,7 +141,7 @@ def tile_deepseekmultiheadattention_pb_t_kernel(
 
         def wb_interleave():
             by_head = wb_raw[:].rearrange("p j (h c) -> p h c j", h=H)
-            nc.scalar.copy(
+            nc.vector.tensor_copy(
                 out=wb_il[:, 0:256, :].rearrange("p (h c) j -> p h c j", h=H), in_=by_head[:, :, NOPE:, :]
             )
             nc.scalar.copy(
@@ -141,7 +152,7 @@ def tile_deepseekmultiheadattention_pb_t_kernel(
             quantize(wb_q[:, 0:256], wb_s[:, 0:256], wb_il[:, 0:256, :].rearrange("p n j -> p (n j)"))
             quantize(wb_q[:, 256:384], wb_s[:, 256:384], wb_il[:, 256:384, :].rearrange("p n j -> p (n j)"))
 
-        def trig_tables():
+        def trig_arguments():
             nc.vector.tensor_tensor(out=mask[:], in0=ident[:, 0:HALF], in1=ident[:, HALF : 2 * HALF], op=ALU.add)
             col = psum.tile([P, 512], F32, name="kvn")
             nc.tensor.transpose(col[:, 0:P], freq[:, 0, :], ident[:])
@@ -150,7 +161,6 @@ def tile_deepseekmultiheadattention_pb_t_kernel(
             nc.vector.tensor_copy(out=wcol[:], in_=col[:, 0 : 2 * P : P])
             arg = keep.tile([P, 320], F32, name="arg")
             argi = keep.tile([P, 320], I32, name="argi")
-            frac = keep.tile([P, 320], F32, name="frac")
             for lo, hi, wi, ph in ((0, 128, 0, 0), (128, 256, 0, 1), (256, 320, 1, 2)):
                 nc.vector.tensor_scalar(
                     out=arg[:, lo:hi], in0=ramp[:, 0 : hi - lo], scalar1=wcol[:, wi : wi + 1],
@@ -158,7 +168,6 @@ def tile_deepseekmultiheadattention_pb_t_kernel(
                 )
             nc.vector.tensor_copy(out=argi[:], in_=arg[:])
             nc.vector.tensor_tensor(out=frac[:], in0=arg[:], in1=argi[:], op=ALU.subtract)
-            nc.scalar.activation(out=trig[:], in_=frac[:], func=ACT.Sin, scale=2.0 * math.pi)
 
         xs, xw, xg, xq, xsc = {}, {}, {}, {}, {}
         cb, ssq, rr, cnb, cw, cg, cq, csc = {}, {}, {}, {}, {}, {}, {}, {}
@@ -263,13 +272,17 @@ def tile_deepseekmultiheadattention_pb_t_kernel(
                 vst[q] = work.tile([P, H, OCT, VD], F32, name="vst")
             return kst[q], vst[q]
 
-        def kv_evac(u):
+        def v_evac(u):
             kt, vt = out_tiles(u // 4)
             i0 = PAIR * (u % 4)
             nc.scalar.copy(
                 out=vt[:, :, i0 : i0 + PAIR, :].rearrange("p h i d -> p i h d"),
                 in_=kvv[u][:].rearrange("p i (h d) -> p i h d", h=H),
             )
+
+        def k_evac(u):
+            kt, vt = out_tiles(u // 4)
+            i0 = PAIR * (u % 4)
             copy = nc.vector.tensor_copy if u == UNITS - 1 else nc.scalar.copy
             copy(
                 out=kt[:, i0 : i0 + PAIR, :].rearrange("p i (s d) -> p i s d", s=3)[:, :, 0:3:2, :],
@@ -280,99 +293,109 @@ def tile_deepseekmultiheadattention_pb_t_kernel(
         o1 = out_1.rearrange("o h (p i) d -> p (o h) i d", p=P)
 
         def store(u):
-            q = u // 4
-            if q == UNITS // 4 - 1:
-                lo, n = PAIR * (u % 4), PAIR
-            elif u % 4 == 3:
-                lo, n = 0, OCT
-            else:
-                return
+            q, last = u // 4, u // 4 == UNITS // 4 - 1
             kt, vt = out_tiles(q)
-            i0 = q * OCT + lo
-            nc.sync.dma_start(out=o1[:, :, i0 : i0 + n, :], in_=vt[:, :, lo : lo + n, :])
-            nc.sync.dma_start(out=o0[0][:, i0 : i0 + n, :], in_=kt[:, lo : lo + n, 0:128])
-            nc.sync.dma_start(out=o0[1][:, i0 : i0 + n, 0:64], in_=kt[:, lo : lo + n, 128:192])
-            nc.sync.dma_start(out=o0[1][:, i0 : i0 + n, 64:128], in_=kt[:, lo : lo + n, 64:128])
+            done = PAIR * (u % 4) + PAIR
+
+            def rows(n):
+                return slice(q * OCT + done - n, q * OCT + done), slice(done - n, done)
+
+            v_rows = PAIR if last else OCT if u % 4 == 3 else 0
+            k_rows = QUAD if last and u % 2 else OCT if u % 4 == 3 else 0
+            if v_rows:
+                hbm, sb = rows(v_rows)
+                nc.sync.dma_start(out=o1[:, :, hbm, :], in_=vt[:, :, sb, :])
+            if k_rows:
+                hbm, sb = rows(k_rows)
+                nc.sync.dma_start(out=o0[0][:, hbm, :], in_=kt[:, sb, 0:128])
+                nc.sync.dma_start(out=o0[1][:, hbm, 0:64], in_=kt[:, sb, 128:192])
+                nc.sync.dma_start(out=o0[1][:, hbm, 64:128], in_=kt[:, sb, 64:128])
 
         prod, rhs = {}, {}
-        STEPS = 2 * SLOTS // OCT
-        step_at = {(7 * s) // 4: s for s in range(STEPS)}
 
         def rope_rhs(q):
-            rhs[q] = work.tile([P, OCT, HALF], F32, name="rhs")
-            t0 = 2 * P + q * OCT
-            nc.vector.tensor_tensor(
-                out=rhs[q][:], in0=trig[:, t0 : t0 + OCT].unsqueeze(2).to_broadcast([P, OCT, HALF]),
-                in1=mask[:].unsqueeze(1).to_broadcast([P, OCT, HALF]), op=ALU.mult,
+            if q >= SLOTS // QUAD:
+                return
+            rhs[q] = work.tile([P, QUAD, HALF], F32, name="rhs", bufs=4)
+            t0 = 2 * P + q * QUAD
+            nc.gpsimd.tensor_tensor(
+                out=rhs[q][:], in0=trig[:, t0 : t0 + QUAD].unsqueeze(2).to_broadcast([P, QUAD, HALF]),
+                in1=mask[:].unsqueeze(1).to_broadcast([P, QUAD, HALF]), op=ALU.mult,
             )
 
         def rope_table(u):
-            if u not in step_at:
-                return
-            q, which = step_at[u] // 2, step_at[u] % 2
+            q, which = u // 2, u % 2
             nc.tensor.matmul(
-                out=kvn[u][:, 256:512], lhsT=trig[:, which * P : (which + 1) * P],
+                out=kvn[u][:, 256:384], lhsT=trig[:, which * P : (which + 1) * P],
                 rhs=rhs[q][:].rearrange("p i j -> p (i j)"), start=True, stop=True,
             )
 
         def rope_products(u):
-            if u not in step_at:
-                return
-            q, which = step_at[u] // 2, step_at[u] % 2
-            m = work.tile([P, OCT, 2, HALF], F32, name="prod%d" % which)
+            q, which = u // 2, u % 2
+            m = work.tile([P, QUAD, 2, HALF], F32, name="prod%d" % which)
             prod[which] = m
             nc.vector.tensor_tensor(
-                out=m[:], in0=kp[:, q * OCT : (q + 1) * OCT, :].rearrange("p i (s j) -> p i s j", s=2),
-                in1=kvn[u][:, 256:512].rearrange("p (i j) -> p i j", j=HALF).unsqueeze(2).to_broadcast([P, OCT, 2, HALF]),
+                out=m[:], in0=kp[:, q * QUAD : (q + 1) * QUAD, :].rearrange("p i (s j) -> p i s j", s=2),
+                in1=kvn[u][:, 256:384].rearrange("p (i j) -> p i j", j=HALF).unsqueeze(2).to_broadcast([P, QUAD, 2, HALF]),
                 op=ALU.mult,
             )
+
+        def rope_sums(u):
+            q, which = u // 2, u % 2
             if which == 1:
-                kt, vt = out_tiles(q)
+                if u + 3 in rr:
+                    pace = work.tile([P, PAIR], F32, name="pace")
+                    nc.gpsimd.tensor_copy(out=pace[:], in_=rr[u + 3][:])
+                kt, vt = out_tiles(u // 4)
+                rows = slice(QUAD * (q % 2), QUAD * (q % 2) + QUAD)
                 nc.gpsimd.tensor_tensor(
-                    out=kt[:, :, 64:96], in0=prod[0][:, :, 0, :], in1=prod[1][:, :, 1, :], op=ALU.subtract
+                    out=kt[:, rows, 64:96], in0=prod[0][:, :, 0, :], in1=prod[1][:, :, 1, :], op=ALU.subtract
                 )
                 nc.gpsimd.tensor_tensor(
-                    out=kt[:, :, 96:128], in0=prod[0][:, :, 1, :], in1=prod[1][:, :, 0, :], op=ALU.add
+                    out=kt[:, rows, 96:128], in0=prod[0][:, :, 1, :], in1=prod[1][:, :, 0, :], op=ALU.add
                 )
-            elif q + 1 < SLOTS // OCT:
-                rope_rhs(q + 1)
+                rope_rhs(q + 3)
 
         stages = [
+            (mx2, -3),
+            (rope_table, -3),
+            (c_evac, -2),
+            (x_transpose, 2),
+            (rope_products, -3),
+            (squares, 0),
+            (c_quantize, -2),
             (c_transpose, -1),
             (x_scale_mul, 3),
-            (c_quantize, -2),
+            (v_evac, -3),
+            (rnorm, 0),
+            (rope_sums, -3),
+            (x_evac, 2),
             (mx1, 1),
-            (rope_products, -3),
-            (x_transpose, 3),
-            (kv_evac, -3),
+            (k_evac, -3),
             (store, -3),
-            (c_evac, -1),
             (c_norm, 0),
-            (squares, 1),
             (x_quantize, 2),
-            (rnorm, 1),
-            (mx2, -2),
-            (rope_table, -2),
-            (x_evac, 3),
         ]
+        trig_arguments()
         nc.scalar.copy(out=scale_rep[:, D : 2 * D], in_=scale_rep[:, 0:D])
-        wc_interleave(nc.scalar.copy, 1)
         for n in range(-3, UNITS + 3):
             for stage, lag in stages:
                 if 0 <= n + lag < UNITS:
                     stage(n + lag)
             if n == -3:
                 wc_interleave(nc.vector.tensor_copy, 0)
-                trig_tables()
-                nc.scalar.activation(out=zeros[:, 0:1], in_=nhalf[:, 0:1], func=ACT.Abs_reciprocal_sqrt)
+                wc_interleave(nc.scalar.copy, 1)
+                nc.scalar.activation(out=trig[:], in_=frac[:], func=ACT.Sin, scale=2.0 * math.pi)
+                for q in range(3):
+                    rope_rhs(q)
+            if n == -2:
+                wc_quantize(0)
+                wc_quantize(1)
+                nc.scalar.activation(out=warm[:], in_=ones[:], func=ACT.Abs_reciprocal_sqrt)
+            if n == -1:
+                wb_interleave()
                 nc.scalar.copy(
                     out=gain[:].rearrange("p (u m e) -> p u m e", u=2, e=2),
                     in_=gain_raw[:].rearrange("p (m u e) -> p u m e", u=2, e=2),
                 )
-            if n == -2:
-                wc_quantize(0)
-                wc_quantize(1)
-                wb_interleave()
-            if n == -1:
                 wb_quantize()
-                rope_rhs(0)

import math
from contextlib import ExitStack

import concourse.mybir as mybir
from concourse.masks import make_identity

F32 = mybir.dt.float32
BF16 = mybir.dt.bfloat16
I32 = mybir.dt.int32
U32 = mybir.dt.uint32
U8 = mybir.dt.uint8
FP8 = mybir.dt.float8_e4m3fn
FP8X4 = mybir.dt.float8_e4m3fn_x4
ALU = mybir.AluOpType
ACT = mybir.ActivationFunctionType

P = 128
T, D, KVR, H, NOPE, ROPE, VD = 8192, 512, 512, 2, 64, 64, 128
HALF = ROPE // 2
EPS = 1.1920928955078125e-07
FLOPS = 2 * T * D * KVR + 2 * T * KVR * H * (NOPE + VD)

SLOTS = T // P
PAIR = 2
UNITS = SLOTS // PAIR
OCT = 8
QUAD = 4
LOADS = [2, 2, 4] + [8] * 7


def turns(x):
    return x - math.floor(x + 0.5)


def tile_deepseekmultiheadattention_pb_t_kernel(
    tc, x_bytes, x_scale, wkv_c, kv_a_norm_w, wkv_b, k_pe, out_0, out_1
):
    nc = tc.nc
    with ExitStack() as ctx:
        keep = ctx.enter_context(tc.tile_pool(name="keep", bufs=1))
        work = ctx.enter_context(tc.tile_pool(name="work", bufs=3))
        psum = ctx.enter_context(tc.psum_pool(name="psum", bufs=1))
        ctx.enter_context(tc.manual_schedule())

        xview = x_bytes.rearrange("o (p i) k -> p (o i k)", p=P)
        scale_rep = keep.tile([P, PAIR * D], F32, name="scale_rep", align_bytes=64)
        nc.sync.dma_start(
            out=scale_rep[:, 0:D], in_=x_scale.rearrange("a b k -> (a b k)").partition_broadcast(P)
        )
        wc_raw = keep.tile([P, 4, KVR], BF16, name="wc_raw", align_bytes=64)
        nc.scalar.dma_start(out=wc_raw[:], in_=wkv_c.rearrange("(p j) n -> p j n", j=4))

        xb = []
        first = []
        start = 0
        for g, n in enumerate(LOADS):
            t = keep.tile([P, n * D], U8, name="xb%d" % g, align_bytes=64)
            xb.append(t)
            first.append(start)
            start += n
        kp = keep.tile([P, SLOTS, ROPE], BF16, name="kp", align_bytes=64)
        kpview = k_pe.rearrange("o (p i) r -> p (o i) r", p=P)
        wb_raw = keep.tile([P, 4, H * (NOPE + VD)], BF16, name="wb_raw", align_bytes=64)
        gain_raw = keep.tile([P, KVR], BF16, name="gain_raw", align_bytes=64)

        def load_x(g):
            nc.sync.dma_start(out=xb[g][:], in_=xview[:, first[g] * D : (first[g] + LOADS[g]) * D])

        load_x(0)
        load_x(1)
        nc.sync.dma_start(out=gain_raw[:], in_=kv_a_norm_w.partition_broadcast(P))
        load_x(2)
        nc.sync.dma_start(out=wb_raw[:], in_=wkv_b.rearrange("(p j) n -> p j n", j=4))
        load_x(3)
        nc.sync.dma_start(out=kp[:, 0:32, :], in_=kpview[:, 0:32, :])
        load_x(4)
        nc.sync.dma_start(out=kp[:, 32:64, :], in_=kpview[:, 32:64, :])
        for g in range(5, len(LOADS)):
            load_x(g)

        ident = keep.tile([P, P], F32, name="ident")
        make_identity(nc, ident[:])
        ones = keep.tile([P, 1], F32, name="ones")
        nc.vector.memset(ones[:], 1.0)
        warm = keep.tile([P, 1], F32, name="warm")
        nc.scalar.activation(out=warm[:], in_=ones[:], func=ACT.Sin)
        freq = keep.tile([P, 2, P], F32, name="freq")
        nc.vector.memset(freq[:], 0.0)
        for j in range(8):
            nc.vector.tensor_scalar(
                out=freq[:, 1, j : j + 1], in0=ones[:], scalar1=10000.0 ** (-j / HALF) / (2.0 * math.pi),
                scalar2=None, op0=ALU.mult,
            )
        for j in range(11):
            nc.vector.tensor_scalar(
                out=freq[:, 0, j : j + 1], in0=ones[:],
                scalar1=turns(SLOTS * 10000.0 ** (-j / HALF) / (2.0 * math.pi)), scalar2=None, op0=ALU.mult,
            )
        for w, f in ((8, 0.1), (16, 0.01)):
            nc.vector.tensor_scalar(
                out=freq[:, 1, w : 2 * w], in0=freq[:, 1, 0:w], scalar1=f, scalar2=None, op0=ALU.mult
            )
        nc.vector.tensor_scalar(
            out=freq[:, 0, 11:HALF], in0=freq[:, 1, 11:HALF], scalar1=float(SLOTS), scalar2=None, op0=ALU.mult
        )
        nc.vector.tensor_copy(out=freq[:, :, HALF : 2 * HALF], in_=freq[:, :, 0:HALF])
        ramp = keep.tile([P, P], F32, name="ramp")
        nc.gpsimd.iota(
            ramp[:], pattern=[[1, P]], base=0, channel_multiplier=0, allow_small_or_imprecise_dtypes=True
        )
        phase = keep.tile([P, 3], F32, name="phase")
        nc.gpsimd.memset(phase[:], 0.0)
        nc.gpsimd.memset(phase[0:32, 0:1], 0.25)
        nc.gpsimd.memset(phase[32:64, 1:2], -0.25)
        nc.gpsimd.memset(phase[0:32, 2:3], 0.25)
        nc.gpsimd.memset(phase[32:64, 2:3], 0.5)
        mask = keep.tile([P, HALF], F32, name="mask")
        trig = keep.tile([P, 320], F32, name="trig")
        gain = keep.tile([P, KVR], BF16, name="gain")
        frac = keep.tile([P, 320], F32, name="frac")

        wc_il = keep.tile([P, KVR, 4], BF16, name="wc_il", align_bytes=64)
        wc_q = keep.tile([P, KVR], U32, name="wc_q", align_bytes=64)
        wc_s = keep.tile([P, KVR], U8, name="wc_s", align_bytes=64)
        wb_il = keep.tile([P, 384, 4], BF16, name="wb_il", align_bytes=64)
        wb_q = keep.tile([P, 384], U32, name="wb_q", align_bytes=64)
        wb_s = keep.tile([P, 384], U8, name="wb_s", align_bytes=64)

        def quantize(codes, scales, src):
            nc.vector.quantize_mx(out=codes.bitcast(FP8X4), scales=scales, in_=src)

        def wc_interleave(copy, u):
            copy(
                out=wc_il[:, u * 256 : (u + 1) * 256, :].rearrange("p (m e) j -> p m e j", e=2),
                in_=wc_raw[:].rearrange("p j (m u e) -> p u m e j", u=2, e=2)[:, u],
            )

        def wc_quantize(u):
            cols = slice(u * 256, (u + 1) * 256)
            quantize(wc_q[:, cols], wc_s[:, cols], wc_il[:, cols, :].rearrange("p n j -> p (n j)"))

        def wb_interleave():
            by_head = wb_raw[:].rearrange("p j (h c) -> p h c j", h=H)
            nc.vector.tensor_copy(
                out=wb_il[:, 0:256, :].rearrange("p (h c) j -> p h c j", h=H), in_=by_head[:, :, NOPE:, :]
            )
            nc.scalar.copy(
                out=wb_il[:, 256:384, :].rearrange("p (h c) j -> p h c j", h=H), in_=by_head[:, :, 0:NOPE, :]
            )

        def wb_quantize():
            quantize(wb_q[:, 0:256], wb_s[:, 0:256], wb_il[:, 0:256, :].rearrange("p n j -> p (n j)"))
            quantize(wb_q[:, 256:384], wb_s[:, 256:384], wb_il[:, 256:384, :].rearrange("p n j -> p (n j)"))

        def trig_arguments():
            nc.vector.tensor_tensor(out=mask[:], in0=ident[:, 0:HALF], in1=ident[:, HALF : 2 * HALF], op=ALU.add)
            col = psum.tile([P, 512], F32, name="kvn")
            nc.tensor.transpose(col[:, 0:P], freq[:, 0, :], ident[:])
            nc.tensor.transpose(col[:, P : 2 * P], freq[:, 1, :], ident[:])
            wcol = keep.tile([P, 2], F32, name="wcol")
            nc.vector.tensor_copy(out=wcol[:], in_=col[:, 0 : 2 * P : P])
            arg = keep.tile([P, 320], F32, name="arg")
            argi = keep.tile([P, 320], I32, name="argi")
            for lo, hi, wi, ph in ((0, 128, 0, 0), (128, 256, 0, 1), (256, 320, 1, 2)):
                nc.vector.tensor_scalar(
                    out=arg[:, lo:hi], in0=ramp[:, 0 : hi - lo], scalar1=wcol[:, wi : wi + 1],
                    scalar2=phase[:, ph : ph + 1], op0=ALU.mult, op1=ALU.add,
                )
            nc.vector.tensor_copy(out=argi[:], in_=arg[:])
            nc.vector.tensor_tensor(out=frac[:], in0=arg[:], in1=argi[:], op=ALU.subtract)

        xs, xw, xg, xq, xsc = {}, {}, {}, {}, {}
        cb, ssq, rr, cnb, cw, cg, cq, csc = {}, {}, {}, {}, {}, {}, {}, {}
        kvv, kvn, kst, vst = {}, {}, {}, {}

        def x_scale_mul(u):
            g = max(i for i in range(len(LOADS)) if first[i] <= PAIR * u)
            off = (PAIR * u - first[g]) * D
            xs[u] = work.tile([P, PAIR * D], BF16, name="xs", align_bytes=64)
            step = D if u == 0 else PAIR * D
            for lo in range(0, PAIR * D, step):
                nc.vector.tensor_tensor(
                    out=xs[u][:, lo : lo + step], in0=xb[g][:, off + lo : off + lo + step].bitcast(FP8),
                    in1=scale_rep[:, 0:step], op=ALU.mult,
                )

        def x_transpose(u):
            xw[u] = psum.tile([P, 4, P], F32, name="xw")
            words = xs[u][:].bitcast(F32)
            for a in range(PAIR):
                for e in range(2):
                    nc.tensor.transpose(
                        xw[u][:, 2 * a + e, :], words[:, a * 256 + e : (a + 1) * 256 : 2], ident[:]
                    )

        def evac_words(dst, src):
            nc.scalar.copy(
                out=dst.bitcast(F32).rearrange("p (a r u) -> p a r u", a=PAIR, u=2),
                in_=src.rearrange("p (a u) r -> p a r u", a=PAIR),
            )

        def x_evac(u):
            xg[u] = work.tile([P, PAIR * D], BF16, name="xg", align_bytes=64)
            evac_words(xg[u][:], xw[u][:])

        def x_quantize(u):
            xq[u] = work.tile([P, 256], U32, name="xq", align_bytes=64)
            xsc[u] = work.tile([P, 256], U8, name="xsc", align_bytes=64)
            quantize(xq[u][:], xsc[u][:], xg[u][:])

        def mx(out, lq, ls, lcols, rq, rs, rcols):
            nc.tensor.matmul_mx(
                out=out, lhsT=lq[:, lcols].bitcast(FP8X4), lhsT_scale=ls[:, lcols],
                rhs=rq[:, rcols].bitcast(FP8X4), rhs_scale=rs[:, rcols], start=True, stop=True,
            )

        def mx1(u):
            cb[u] = []
            for a in range(PAIR):
                c = psum.tile([P, KVR], F32, name="c", bufs=4)
                mx(c[:], xq[u], xsc[u], slice(a * P, (a + 1) * P), wc_q, wc_s, slice(0, KVR))
                cb[u].append(c)

        def squares(u):
            ssq[u] = work.tile([P, PAIR], F32, name="ssq")
            for a in range(PAIR):
                junk = work.tile([P, KVR], BF16, name="junk")
                nc.scalar.activation(
                    out=junk[:], in_=cb[u][a][:], func=ACT.Square, accum_out=ssq[u][:, a : a + 1]
                )

        def rnorm(u):
            rr[u] = work.tile([P, PAIR], F32, name="rr")
            nc.scalar.activation(
                out=rr[u][:], in_=ssq[u][:], func=ACT.Abs_reciprocal_sqrt, scale=1.0 / KVR, bias=EPS
            )

        def c_norm(u):
            cnb[u] = work.tile([P, PAIR * KVR], BF16, name="cnb", align_bytes=64)
            for a in range(PAIR):
                nc.vector.scalar_tensor_tensor(
                    out=cnb[u][:, a * KVR : (a + 1) * KVR], in0=cb[u][a][:], scalar=rr[u][:, a : a + 1],
                    in1=gain[:], op0=ALU.mult, op1=ALU.mult,
                )

        def c_transpose(u):
            cw[u] = psum.tile([P, 4, P], F32, name="cw")
            words = cnb[u][:].bitcast(F32)
            for b in range(4):
                nc.tensor.transpose(cw[u][:, b, :], words[:, b * P : (b + 1) * P], ident[:])

        def c_evac(u):
            cg[u] = work.tile([P, PAIR * KVR], BF16, name="cg", align_bytes=64)
            evac_words(cg[u][:], cw[u][:])

        def c_quantize(u):
            cq[u] = work.tile([P, 256], U32, name="cq", align_bytes=64)
            csc[u] = work.tile([P, 256], U8, name="csc", align_bytes=64)
            quantize(cq[u][:], csc[u][:], cg[u][:])

        def mx2(u):
            kvv[u] = psum.tile([P, PAIR, 256], F32, name="kvv")
            kvn[u] = psum.tile([P, 512], F32, name="kvn")
            for a in range(PAIR):
                cols = slice(a * P, (a + 1) * P)
                mx(kvv[u][:, a, :], cq[u], csc[u], cols, wb_q, wb_s, slice(0, 256))
                mx(kvn[u][:, a * P : (a + 1) * P], cq[u], csc[u], cols, wb_q, wb_s, slice(256, 384))

        def out_tiles(q):
            if q not in kst:
                kst[q] = work.tile([P, OCT, 192], F32, name="kst")
                vst[q] = work.tile([P, H, OCT, VD], F32, name="vst")
            return kst[q], vst[q]

        def v_evac(u):
            kt, vt = out_tiles(u // 4)
            i0 = PAIR * (u % 4)
            nc.scalar.copy(
                out=vt[:, :, i0 : i0 + PAIR, :].rearrange("p h i d -> p i h d"),
                in_=kvv[u][:].rearrange("p i (h d) -> p i h d", h=H),
            )

        def k_evac(u):
            kt, vt = out_tiles(u // 4)
            i0 = PAIR * (u % 4)
            copy = nc.vector.tensor_copy if u == UNITS - 1 else nc.scalar.copy
            copy(
                out=kt[:, i0 : i0 + PAIR, :].rearrange("p i (s d) -> p i s d", s=3)[:, :, 0:3:2, :],
                in_=kvn[u][:, 0:256].rearrange("p (i h d) -> p i h d", i=PAIR, h=H),
            )

        o0 = out_0.rearrange("o h (p i) d -> (o h) p i d", p=P)
        o1 = out_1.rearrange("o h (p i) d -> p (o h) i d", p=P)

        def store(u):
            q, last = u // 4, u // 4 == UNITS // 4 - 1
            kt, vt = out_tiles(q)
            done = PAIR * (u % 4) + PAIR

            def rows(n):
                return slice(q * OCT + done - n, q * OCT + done), slice(done - n, done)

            v_rows = PAIR if last else OCT if u % 4 == 3 else 0
            k_rows = QUAD if last and u % 2 else OCT if u % 4 == 3 else 0
            if v_rows:
                hbm, sb = rows(v_rows)
                nc.sync.dma_start(out=o1[:, :, hbm, :], in_=vt[:, :, sb, :])
            if k_rows:
                hbm, sb = rows(k_rows)
                nc.sync.dma_start(out=o0[0][:, hbm, :], in_=kt[:, sb, 0:128])
                nc.sync.dma_start(out=o0[1][:, hbm, 0:64], in_=kt[:, sb, 128:192])
                nc.sync.dma_start(out=o0[1][:, hbm, 64:128], in_=kt[:, sb, 64:128])

        prod, rhs = {}, {}

        def rope_rhs(q):
            if q >= SLOTS // QUAD:
                return
            rhs[q] = work.tile([P, QUAD, HALF], F32, name="rhs", bufs=4)
            t0 = 2 * P + q * QUAD
            nc.gpsimd.tensor_tensor(
                out=rhs[q][:], in0=trig[:, t0 : t0 + QUAD].unsqueeze(2).to_broadcast([P, QUAD, HALF]),
                in1=mask[:].unsqueeze(1).to_broadcast([P, QUAD, HALF]), op=ALU.mult,
            )

        def rope_table(u):
            q, which = u // 2, u % 2
            nc.tensor.matmul(
                out=kvn[u][:, 256:384], lhsT=trig[:, which * P : (which + 1) * P],
                rhs=rhs[q][:].rearrange("p i j -> p (i j)"), start=True, stop=True,
            )

        def rope_products(u):
            q, which = u // 2, u % 2
            m = work.tile([P, QUAD, 2, HALF], F32, name="prod%d" % which)
            prod[which] = m
            nc.vector.tensor_tensor(
                out=m[:], in0=kp[:, q * QUAD : (q + 1) * QUAD, :].rearrange("p i (s j) -> p i s j", s=2),
                in1=kvn[u][:, 256:384].rearrange("p (i j) -> p i j", j=HALF).unsqueeze(2).to_broadcast([P, QUAD, 2, HALF]),
                op=ALU.mult,
            )

        def rope_sums(u):
            q, which = u // 2, u % 2
            if which == 1:
                if u + 3 in rr:
                    pace = work.tile([P, PAIR], F32, name="pace")
                    nc.gpsimd.tensor_copy(out=pace[:], in_=rr[u + 3][:])
                kt, vt = out_tiles(u // 4)
                rows = slice(QUAD * (q % 2), QUAD * (q % 2) + QUAD)
                nc.gpsimd.tensor_tensor(
                    out=kt[:, rows, 64:96], in0=prod[0][:, :, 0, :], in1=prod[1][:, :, 1, :], op=ALU.subtract
                )
                nc.gpsimd.tensor_tensor(
                    out=kt[:, rows, 96:128], in0=prod[0][:, :, 1, :], in1=prod[1][:, :, 0, :], op=ALU.add
                )
                rope_rhs(q + 3)

        stages = [
            (mx2, -3),
            (rope_table, -3),
            (c_evac, -2),
            (x_transpose, 2),
            (rope_products, -3),
            (squares, 0),
            (c_quantize, -2),
            (c_transpose, -1),
            (x_scale_mul, 3),
            (v_evac, -3),
            (rnorm, 0),
            (rope_sums, -3),
            (x_evac, 2),
            (mx1, 1),
            (k_evac, -3),
            (store, -3),
            (c_norm, 0),
            (x_quantize, 2),
        ]
        trig_arguments()
        nc.scalar.copy(out=scale_rep[:, D : 2 * D], in_=scale_rep[:, 0:D])
        for n in range(-3, UNITS + 3):
            for stage, lag in stages:
                if 0 <= n + lag < UNITS:
                    stage(n + lag)
            if n == -3:
                wc_interleave(nc.vector.tensor_copy, 0)
                wc_interleave(nc.scalar.copy, 1)
                nc.scalar.activation(out=trig[:], in_=frac[:], func=ACT.Sin, scale=2.0 * math.pi)
                for q in range(3):
                    rope_rhs(q)
            if n == -2:
                wc_quantize(0)
                wc_quantize(1)
                nc.scalar.activation(out=warm[:], in_=ones[:], func=ACT.Abs_reciprocal_sqrt)
            if n == -1:
                wb_interleave()
                nc.scalar.copy(
                    out=gain[:].rearrange("p (u m e) -> p u m e", u=2, e=2),
                    in_=gain_raw[:].rearrange("p (m u e) -> p u m e", u=2, e=2),
                )
                wb_quantize()
